import numpy as np
import ml_dtypes


def mxq(x, axis, fmt="e4m3"):
    dtype, down = {"e4m3": (ml_dtypes.float8_e4m3fn, 7), "e5m2": (ml_dtypes.float8_e5m2, 14)}[fmt]
    v = np.moveaxis(np.asarray(x, np.float32).astype(ml_dtypes.bfloat16).astype(np.float64), axis, -1)
    blocks = v.reshape(v.shape[:-1] + (-1, 32))
    amax = np.abs(blocks).max(-1, keepdims=True)
    byte = np.maximum(np.where(amax > 0, np.frexp(amax)[1] - 1 + 127, 0) - down, 1)
    scale = np.exp2(byte - 127.0)
    codes = (blocks / scale).astype(np.float32).astype(dtype).astype(np.float64)
    return np.moveaxis((codes * scale).reshape(v.shape), -1, axis)


WIDE = False


def mx_kscale(k):
    if not WIDE:
        return np.ones(k)
    levels = np.array([30, -30])
    if k % 512:
        return np.exp2(np.random.permutation(np.resize(levels, k // 32))).repeat(32)
    a = np.empty((k // 512, 16))
    for p in range(k // 512):
        a[p, :8] = np.random.permutation(np.resize(levels, 8))
        for g in range(8):
            far = levels[np.abs(levels - a[p, g]) >= 10]
            a[p, g + 8] = far[np.random.randint(len(far))]
    return np.exp2(a.ravel()).repeat(32)


BF16 = ml_dtypes.bfloat16


def bf(x):
    return np.asarray(x, np.float32).astype(BF16)


def f64(x):
    return np.asarray(x).astype(np.float64)


E2M1 = np.array([0.0, 0.5, 1.0, 1.5, 2.0, 3.0, 4.0, 6.0, -0.0, -0.5, -1.0, -1.5, -2.0, -3.0, -4.0, -6.0])


def pack_weight(w, fmt):
    k, n = w.shape
    w = f64(bf(w)).reshape(k // 32, 32, n)
    amax = np.abs(w).max(1)
    if fmt == "e4m3":
        byte = np.frexp(amax)[1] - 1 + 127 - 7
    else:
        mant, ex = np.frexp(amax / 6.0)
        byte = np.where(mant > 0.5, ex, ex - 1) + 127
    byte = np.clip(np.where(amax > 0, byte, 1), 1, 254)
    scaled = (w * np.exp2(127.0 - byte)[:, None, :]).reshape(k, n).astype(np.float32)
    by_word = np.ascontiguousarray(scaled.reshape(k // 512, 128, 4, n).transpose(0, 1, 3, 2))
    if fmt == "e4m3":
        words = by_word.astype(ml_dtypes.float8_e4m3fn).view(np.uint8)
    else:
        c = by_word.astype(ml_dtypes.float4_e2m1fn).view(np.uint8) & 0xF
        words = c[..., 0::2] | (c[..., 1::2] << 4)
    return np.ascontiguousarray(words), np.ascontiguousarray(byte.astype(np.uint8).reshape(k // 512, 16, n))


def unpack_weight(words, scales, fmt):
    g, p, n, _ = words.shape
    if fmt == "e4m3":
        vals = np.ascontiguousarray(words).view(ml_dtypes.float8_e4m3fn).astype(np.float64)
    else:
        nib = np.empty((g, p, n, 4), np.uint8)
        nib[..., 0::2] = words & 0xF
        nib[..., 1::2] = words >> 4
        vals = E2M1[nib]
    vals = vals * np.repeat(np.exp2(scales.astype(np.float64) - 127.0), 8, axis=1)[..., None]
    return vals.transpose(0, 1, 3, 2).reshape(g * 512, n)

def pack4(w):
    words, scales = pack_weight(w, "e2m1")
    return words.reshape(words.shape[0], 128, -1), scales


def unpack4(words, scales):
    return unpack_weight(words.reshape(words.shape[0], 128, -1, 2), scales, "e2m1")


S, D, H = 1024, 1024, 16
DH = D // H
HALF = DH // 2
MAX_WAVELENGTH = 10000.0


def rope(t):
    fraction = 2.0 * np.arange(HALF) / DH
    timescale = MAX_WAVELENGTH ** fraction
    ang = np.arange(S)[:, None] / timescale[None, :]
    sin, cos = np.sin(ang), np.cos(ang)
    first, second = t[..., :HALF], t[..., HALF:]
    return np.concatenate([first * cos - second * sin, second * cos + first * sin], axis=-1)


def setup_inputs():
    s = mx_kscale(D)
    x = bf(np.random.standard_normal((S, D)) * s)
    words, scales = pack4(np.random.standard_normal((D, 3 * D)) / np.sqrt(D) / s[:, None])
    b_kqv = bf(np.random.standard_normal(3 * D) * 0.2)
    return {"x": x,
            "W_kqv_words": words,
            "W_kqv_scales": scales,
            "b_kqv": b_kqv}


def reference(x, W_kqv_words, W_kqv_scales, b_kqv):
    qkv = (mxq(f64(x), 1, "e5m2") @ unpack4(W_kqv_words, W_kqv_scales)) + f64(b_kqv)
    qkv = qkv.reshape(S, 3, H, DH).transpose(1, 2, 0, 3)
    return rope(qkv[0]), rope(qkv[1]), qkv[2]

@@ -1,0 +1,295 @@
+import math
+from contextlib import ExitStack
+
+import concourse.mybir as mybir
+from concourse.masks import make_identity
+
+S, D, H, DH = 1024, 1024, 16, 64
+HALF = DH // 2
+FLOPS = 2 * S * D * 3 * D
+
+F32 = mybir.dt.float32
+BF16 = mybir.dt.bfloat16
+I32 = mybir.dt.int32
+U32 = mybir.dt.uint32
+U8 = mybir.dt.uint8
+E5M2X4 = mybir.dt.float8_e5m2_x4
+E2M1X4 = mybir.dt.float4_e2m1fn_x4
+ALU = mybir.AluOpType
+ACT = mybir.ActivationFunctionType
+
+P = 128
+PASSES = D // 512
+BANK = 512
+SUB = 4
+SPAN = P * SUB
+SPANS = S // SPAN
+W_TILES = 3 * D // BANK
+QK_TILES = 2 * D // P
+UNITS_PER_SPAN = QK_TILES // 2
+
+
+def tile_attention_pa_kernel(tc, x, W_kqv_words, W_kqv_scales, b_kqv, out_0, out_1, out_2):
+    nc = tc.nc
+    with ExitStack() as ctx:
+        keep = ctx.enter_context(tc.tile_pool(name="keep", bufs=1))
+        work = ctx.enter_context(tc.tile_pool(name="work", bufs=3))
+        psum = ctx.enter_context(tc.psum_pool(name="psum", bufs=4))
+        ctx.enter_context(tc.manual_schedule())
+
+        ident = keep.tile([P, P], F32, name="ident")
+        ident_bf = keep.tile([P, P], BF16, name="ident_bf")
+        bias_rows = keep.tile([P, P], BF16, name="bias_rows")
+        bias_col = keep.tile([P, QK_TILES], F32, name="bias_col")
+        bias_v = keep.tile([P, D], F32, name="bias_v")
+        w_scales = keep.tile([P, PASSES, 3 * D], U8, name="w_scales", align_bytes=64)
+        w_words = [keep.tile([P, PASSES, 2 * BANK], U8, name="w_words%d" % c, align_bytes=64) for c in range(W_TILES)]
+        x_rows = {}
+        x_codes = [keep.tile([P, PASSES, SPAN], U32, name="x_codes%d" % s, align_bytes=64) for s in range(SPANS)]
+        x_scales = [keep.tile([P, PASSES, SPAN], U8, name="x_scales%d" % s, align_bytes=64) for s in range(SPANS)]
+        token = keep.tile([P, SPANS * SUB], F32, name="token")
+        turns = keep.tile([P, SPANS * SUB, HALF], F32, name="turns")
+        whole = keep.tile([P, SPANS * SUB, HALF], I32, name="whole")
+        frac = keep.tile([P, SPANS * SUB, HALF], F32, name="frac")
+        folded = keep.tile([P, SPANS * SUB, HALF], F32, name="folded")
+        cos_t = keep.tile([P, SPANS * SUB, 2, HALF], F32, name="cos_t")
+        sin_t = keep.tile([P, SPANS * SUB, 2, HALF], F32, name="sin_t")
+
+        w_hbm = W_kqv_words.rearrange("g p b -> p g b")
+
+        def load_x(s, j0, count):
+            rows = x[s * SPAN : (s + 1) * SPAN, :].rearrange("(p j) k -> p j k", j=SUB)
+            loaded = keep.tile([P, count, D], BF16, name="x_rows%d_%d" % (s, j0))
+            nc.sync.dma_start(out=loaded[:], in_=rows[:, j0 : j0 + count, :])
+            for j in range(count):
+                x_rows[s, j0 + j] = loaded[:, j, :]
+
+        def load_w(c):
+            nc.sync.dma_start(
+                out=w_words[c][:].bitcast(I32), in_=w_hbm[:, :, 2 * BANK * c : 2 * BANK * (c + 1)].bitcast(I32)
+            )
+
+        nc.vector.memset(bias_rows[:], 0.0)
+        nc.vector.memset(w_scales[:].bitcast(I32), 0)
+        nc.gpsimd.iota(
+            token[:], pattern=[[SPAN, SPANS], [1, SUB]], base=0, channel_multiplier=SUB,
+            allow_small_or_imprecise_dtypes=True,
+        )
+        nc.gpsimd.dma_start(out=bias_rows[0 : 3 * D // P, :], in_=b_kqv.rearrange("(r c) -> r c", c=P))
+        make_identity(nc, ident[:])
+        make_identity(nc, ident_bf[:])
+        load_x(0, 0, 1)
+        load_x(0, 1, 1)
+        load_x(0, 2, 2)
+        load_w(4)
+        for q in (0, 2, 1, 3):
+            nc.sync.dma_start(
+                out=w_scales[32 * q : 32 * q + 4, :, :].bitcast(I32),
+                in_=W_kqv_scales[:, 4 * q : 4 * q + 4, :].rearrange("g r n -> r g n").bitcast(I32),
+            )
+        load_w(0)
+        load_w(1)
+        load_x(1, 0, 2)
+        load_x(1, 2, 2)
+        load_w(5)
+        load_w(2)
+        load_w(3)
+
+        nc.vector.tensor_scalar(
+            out=turns[:, :, 0], in0=token[:], scalar1=1.0 / (2.0 * math.pi), scalar2=None, op0=ALU.mult
+        )
+        width = 1
+        while width < HALF:
+            nc.vector.tensor_scalar(
+                out=turns[:, :, width : 2 * width], in0=turns[:, :, 0:width],
+                scalar1=10000.0 ** (-width / HALF), scalar2=None, op0=ALU.mult,
+            )
+            width *= 2
+        nc.vector.tensor_copy(out=whole[:], in_=turns[:])
+        nc.vector.tensor_tensor(out=frac[:], in0=turns[:], in1=whole[:], op=ALU.subtract)
+        nc.vector.scalar_tensor_tensor(
+            out=folded[:], in0=frac[:], scalar=-1.0, in1=frac[:], op0=ALU.mult, op1=ALU.min
+        )
+        nc.vector.tensor_scalar(out=folded[:], in0=folded[:], scalar1=0.25, scalar2=None, op0=ALU.add)
+
+        def trig_tables():
+            two_pi = 2.0 * math.pi
+            nc.scalar.activation(
+                out=cos_t[:], in_=folded[:].unsqueeze(2).broadcast_to([P, SPANS * SUB, 2, HALF]),
+                func=ACT.Sin, scale=two_pi,
+            )
+            nc.scalar.activation(out=sin_t[:, :, 0, :], in_=frac[:], func=ACT.Sin, scale=-two_pi)
+            nc.scalar.activation(out=sin_t[:, :, 1, :], in_=frac[:], func=ACT.Sin, scale=two_pi)
+
+        def transpose_x(s, j):
+            words = x_rows[s, j].bitcast(F32)
+            tag = "tb" if s == 0 else "mx"
+            bank = psum.tile([P, PASSES, 2, P], F32, name=tag, tag=tag)
+            for g in range(PASSES):
+                for u in range(2):
+                    nc.tensor.transpose(bank[:, g, u, :], words[:, 256 * g + u : 256 * (g + 1) : 2], ident[:])
+            grouped = work.tile([P, PASSES, 4 * P], BF16, name="grouped", tag="grouped", bufs=4, align_bytes=64)
+            nc.scalar.copy(
+                out=grouped[:].bitcast(F32).rearrange("p g (r u) -> p g r u", u=2),
+                in_=bank[:].rearrange("p g u r -> p g r u"),
+            )
+            return grouped
+
+        def quantize_x(s, j, grouped):
+            cols = slice(j * P, (j + 1) * P)
+            for g in range(PASSES):
+                nc.vector.quantize_mx(
+                    out=x_codes[s][:, g, cols].bitcast(E5M2X4), scales=x_scales[s][:, g, cols], in_=grouped[:, g, :]
+                )
+
+        def spread_bias():
+            bank = psum.tile([P, BANK], F32, name="mx", tag="mx")
+            nc.tensor.matmul(bank[:, 0:QK_TILES], lhsT=bias_rows[:], rhs=ident_bf[:, 0:QK_TILES], start=True, stop=True)
+            nc.scalar.copy(out=bias_col[:], in_=bank[:, 0:QK_TILES])
+            for c in range(2):
+                bank = psum.tile([P, BANK], F32, name="mx", tag="mx")
+                for r in range(4):
+                    row = QK_TILES + 4 * c + r
+                    nc.tensor.matmul(
+                        bank[:, r * P : (r + 1) * P], lhsT=ident_bf[:, row : row + 1].to_broadcast([P, P]),
+                        rhs=bias_rows[:], start=True, stop=True,
+                    )
+                nc.scalar.copy(out=bias_v[:, c * BANK : (c + 1) * BANK], in_=bank[:])
+
+        v_out = {}
+
+        def v_product(s, c, j):
+            bank = psum.tile([P, BANK], F32, name="mx", tag="mx")
+            cols = slice(j * P, (j + 1) * P)
+            wt = 4 + c
+            for g in range(PASSES):
+                nc.tensor.matmul_mx(
+                    out=bank[:],
+                    lhsT=x_codes[s][:, g, cols].bitcast(E5M2X4), lhsT_scale=x_scales[s][:, g, cols],
+                    rhs=w_words[wt][:, g, :].bitcast(E2M1X4), rhs_scale=w_scales[:, g, wt * BANK : (wt + 1) * BANK],
+                    start=(g == 0), stop=(g == PASSES - 1),
+                )
+            return bank
+
+        def v_finish(s, c, j, bank):
+            if j == 0:
+                v_out[s, c] = work.tile([P, 8, SUB, DH], F32, name="v_out", tag="v_out", bufs=2)
+            nc.vector.tensor_tensor(
+                out=v_out[s, c][:, :, j, :], in0=bank[:].rearrange("p (h f) -> p h f", f=DH),
+                in1=bias_v[:, c * BANK : (c + 1) * BANK].rearrange("p (h f) -> p h f", f=DH), op=ALU.add,
+            )
+            hbm = out_2[8 * c : 8 * (c + 1), s * SPAN : (s + 1) * SPAN, :].rearrange("h (p j) f -> p h (j f)", j=SUB)
+            if j % 2 == 1:
+                run = slice((j - 1) * DH, (j + 1) * DH)
+                nc.sync.dma_start(out=hbm[:, :, run], in_=v_out[s, c][:].rearrange("p h j f -> p h (j f)")[:, :, run])
+
+        biased = {}
+
+        def qk_product(n):
+            s, pair = divmod(n, UNITS_PER_SPAN)
+            for e in range(2):
+                m = 2 * pair + e
+                bank = psum.tile([P, BANK], F32, name="mx", tag="mx")
+                wt, part = divmod(m, 4)
+                for g in range(PASSES):
+                    nc.tensor.matmul_mx(
+                        out=bank[:],
+                        lhsT=w_words[wt][:, g, 2 * P * part : 2 * P * (part + 1)].bitcast(E2M1X4),
+                        lhsT_scale=w_scales[:, g, m * P : (m + 1) * P],
+                        rhs=x_codes[s][:, g, :].bitcast(E5M2X4), rhs_scale=x_scales[s][:, g, :],
+                        start=(g == 0), stop=(g == PASSES - 1),
+                    )
+                biased[n, e] = work.tile([P, BANK], F32, name="biased", tag="biased", bufs=4)
+                nc.scalar.activation(
+                    out=biased[n, e][:], in_=bank[:], func=ACT.Identity, bias=bias_col[:, m : m + 1], scale=1.0
+                )
+
+        def qk_turn(n):
+            banks = []
+            for e in range(2):
+                bank = psum.tile([P, SUB, 2, DH], F32, name="tb", tag="tb")
+                for j in range(SUB):
+                    nc.tensor.transpose(
+                        bank[:, j, :, :].rearrange("p h f -> p (h f)"), biased[n, e][:, j * P : (j + 1) * P], ident[:]
+                    )
+                banks.append(bank)
+            return banks
+
+        def qk_rotate(n, banks):
+            s, pair = divmod(n, UNITS_PER_SPAN)
+            rows = slice(s * SUB, (s + 1) * SUB)
+            by_cos = work.tile([P, 4, SUB, DH], F32, name="by_cos", tag="by_cos")
+            by_sin = work.tile([P, 4, SUB, DH], F32, name="by_sin", tag="by_sin")
+            for e in range(2):
+                t = banks[e][:].rearrange("p j h f -> p h j f")
+                heads = slice(2 * e, 2 * e + 2)
+                nc.vector.tensor_tensor(
+                    out=by_cos[:, heads, :, :], in0=t,
+                    in1=cos_t[:, rows, :, :].rearrange("p j a i -> p j (a i)").unsqueeze(1).broadcast_to([P, 2, SUB, DH]),
+                    op=ALU.mult,
+                )
+                nc.vector.tensor_tensor(
+                    out=by_sin[:, heads, :, :].rearrange("p h j (a i) -> p j h a i", a=2),
+                    in0=banks[e][:].rearrange("p j h (a i) -> p j h a i", a=2)[:, :, :, ::-1, :],
+                    in1=sin_t[:, rows, :, :].unsqueeze(2).broadcast_to([P, SUB, 2, 2, HALF]),
+                    op=ALU.mult,
+                )
+            return by_cos, by_sin
+
+        def qk_add(n, by_cos, by_sin, heads):
+            rotated = work.tile([P, 4, SUB * DH], F32, name="rotated", tag="rotated", bufs=4)
+            nc.gpsimd.tensor_tensor(
+                out=rotated[:, heads, :].rearrange("p h r -> p (h r)"),
+                in0=by_cos[:, heads, :, :].rearrange("p h j f -> p (h j f)"),
+                in1=by_sin[:, heads, :, :].rearrange("p h j f -> p (h j f)"), op=ALU.add,
+            )
+            return rotated
+
+        def qk_store(n, rotated, heads):
+            s, pair = divmod(n, UNITS_PER_SPAN)
+            which, group = divmod(pair, 4)
+            hbm = (out_0, out_1)[which][4 * group : 4 * (group + 1), s * SPAN : (s + 1) * SPAN, :]
+            nc.sync.dma_start(out=hbm.rearrange("h (p j) f -> p h (j f)", j=SUB)[:, heads, :], in_=rotated[:, heads, :])
+
+        groups = [transpose_x(0, 0), transpose_x(0, 1)]
+        spread_bias()
+        groups += [transpose_x(0, 2), transpose_x(0, 3)]
+        trig_tables()
+        quantize_x(0, 0, groups[0])
+        quantize_x(0, 1, groups[1])
+        v_banks = [v_product(0, 0, 0), v_product(0, 0, 1)]
+        quantize_x(0, 2, groups[2])
+        quantize_x(0, 3, groups[3])
+        v_finish(0, 0, 0, v_banks[0])
+        v_finish(0, 0, 1, v_banks[1])
+        qk_product(0)
+        for j in range(2, SUB):
+            v_finish(0, 0, j, v_product(0, 0, j))
+
+        units = SPANS * UNITS_PER_SPAN
+        all_heads = slice(0, 4)
+        v_in_step = {1: (0, 1, 0), 6: (0, 1, 1), 7: (0, 1, 2), 8: (0, 1, 3),
+                     9: (1, 0, 0), 10: (1, 0, 1), 12: (1, 0, 2), 14: (1, 0, 3)}
+        x_in_step = {2: 0, 3: 1, 4: 2, 5: 3}
+        for n in range(units):
+            if n == 1:
+                qk_product(1)
+            if 0 < n < units - 1:
+                qk_product(n + 1)
+            v_bank = v_product(*v_in_step[n]) if n in v_in_step else None
+            banks = qk_turn(n)
+            grouped = transpose_x(1, x_in_step[n]) if n in x_in_step else None
+            by_cos, by_sin = qk_rotate(n, banks)
+            if n < units - 1:
+                qk_store(n, qk_add(n, by_cos, by_sin, all_heads), all_heads)
+            if grouped is not None:
+                quantize_x(1, x_in_step[n], grouped)
+            if v_bank is not None:
+                v_finish(*v_in_step[n], v_bank)
+        last = [v_product(1, 1, j) for j in range(SUB)]
+        for e in range(2):
+            heads = slice(2 * e, 2 * e + 2)
+            rotated = qk_add(units - 1, by_cos, by_sin, heads)
+            for j in range(2 * e, 2 * e + 2):
+                v_finish(1, 1, j, last[j])
+            qk_store(units - 1, rotated, heads)

@@ -2,7 +2,6 @@ import math
 from contextlib import ExitStack
 
 import concourse.mybir as mybir
-from concourse.masks import make_identity
 
 S, D, H, DH = 1024, 1024, 16, 64
 HALF = DH // 2
@@ -37,10 +36,11 @@ def tile_attention_pa_kernel(tc, x, W_kqv_words, W_kqv_scales, b_kqv, out_0, out
         psum = ctx.enter_context(tc.psum_pool(name="psum", bufs=4))
         ctx.enter_context(tc.manual_schedule())
 
+        offset = keep.tile([P, P], F32, name="offset")
         ident = keep.tile([P, P], F32, name="ident")
         ident_bf = keep.tile([P, P], BF16, name="ident_bf")
         bias_rows = keep.tile([P, P], BF16, name="bias_rows")
-        bias_col = keep.tile([P, QK_TILES], F32, name="bias_col")
+        bias_col = keep.tile([P, 3 * D // P], F32, name="bias_col")
         bias_v = keep.tile([P, D], F32, name="bias_v")
         w_scales = keep.tile([P, PASSES, 3 * D], U8, name="w_scales", align_bytes=64)
         w_words = [keep.tile([P, PASSES, 2 * BANK], U8, name="w_words%d" % c, align_bytes=64) for c in range(W_TILES)]
@@ -70,41 +70,44 @@ def tile_attention_pa_kernel(tc, x, W_kqv_words, W_kqv_scales, b_kqv, out_0, out
             )
 
         nc.vector.memset(bias_rows[:], 0.0)
-        nc.vector.memset(w_scales[:].bitcast(I32), 0)
+        nc.gpsimd.iota(
+            offset[:], pattern=[[1, P]], base=0, channel_multiplier=-1, allow_small_or_imprecise_dtypes=True
+        )
         nc.gpsimd.iota(
             token[:], pattern=[[SPAN, SPANS], [1, SUB]], base=0, channel_multiplier=SUB,
             allow_small_or_imprecise_dtypes=True,
         )
-        nc.gpsimd.dma_start(out=bias_rows[0 : 3 * D // P, :], in_=b_kqv.rearrange("(r c) -> r c", c=P))
-        make_identity(nc, ident[:])
-        make_identity(nc, ident_bf[:])
+        for eye in (ident_bf, ident):
+            nc.vector.tensor_scalar(out=eye[:], in0=offset[:], scalar1=0.0, scalar2=None, op0=ALU.is_equal)
+        nc.vector.memset(w_scales[:].bitcast(I32), 0)
+        nc.scalar.dma_start(out=bias_rows[0 : 3 * D // P, :], in_=b_kqv.rearrange("(r c) -> r c", c=P))
         load_x(0, 0, 1)
         load_x(0, 1, 1)
         load_x(0, 2, 2)
-        load_w(4)
         for q in (0, 2, 1, 3):
             nc.sync.dma_start(
                 out=w_scales[32 * q : 32 * q + 4, :, :].bitcast(I32),
                 in_=W_kqv_scales[:, 4 * q : 4 * q + 4, :].rearrange("g r n -> r g n").bitcast(I32),
             )
+        load_w(4)
         load_w(0)
-        load_w(1)
         load_x(1, 0, 2)
         load_x(1, 2, 2)
+        load_w(1)
         load_w(5)
         load_w(2)
         load_w(3)
 
-        nc.vector.tensor_scalar(
-            out=turns[:, :, 0], in0=token[:], scalar1=1.0 / (2.0 * math.pi), scalar2=None, op0=ALU.mult
-        )
-        width = 1
-        while width < HALF:
+        for i in range(4):
             nc.vector.tensor_scalar(
-                out=turns[:, :, width : 2 * width], in0=turns[:, :, 0:width],
-                scalar1=10000.0 ** (-width / HALF), scalar2=None, op0=ALU.mult,
+                out=turns[:, :, i], in0=token[:], scalar1=10000.0 ** (-i / HALF) / (2.0 * math.pi), scalar2=None,
+                op0=ALU.mult,
             )
-            width *= 2
+        for i in range(4, HALF, 4):
+            nc.vector.tensor_scalar(
+                out=turns[:, :, i : i + 4], in0=turns[:, :, 0:4], scalar1=10000.0 ** (-i / HALF), scalar2=None,
+                op0=ALU.mult,
+            )
         nc.vector.tensor_copy(out=whole[:], in_=turns[:])
         nc.vector.tensor_tensor(out=frac[:], in0=turns[:], in1=whole[:], op=ALU.subtract)
         nc.vector.scalar_tensor_tensor(
@@ -121,32 +124,31 @@ def tile_attention_pa_kernel(tc, x, W_kqv_words, W_kqv_scales, b_kqv, out_0, out
             nc.scalar.activation(out=sin_t[:, :, 0, :], in_=frac[:], func=ACT.Sin, scale=-two_pi)
             nc.scalar.activation(out=sin_t[:, :, 1, :], in_=frac[:], func=ACT.Sin, scale=two_pi)
 
-        def transpose_x(s, j):
+        def transpose_x(s, j, grouped):
             words = x_rows[s, j].bitcast(F32)
             tag = "tb" if s == 0 else "mx"
             bank = psum.tile([P, PASSES, 2, P], F32, name=tag, tag=tag)
             for g in range(PASSES):
                 for u in range(2):
                     nc.tensor.transpose(bank[:, g, u, :], words[:, 256 * g + u : 256 * (g + 1) : 2], ident[:])
-            grouped = work.tile([P, PASSES, 4 * P], BF16, name="grouped", tag="grouped", bufs=4, align_bytes=64)
             nc.scalar.copy(
-                out=grouped[:].bitcast(F32).rearrange("p g (r u) -> p g r u", u=2),
+                out=grouped.bitcast(F32).rearrange("p g (r u) -> p g r u", u=2),
                 in_=bank[:].rearrange("p g u r -> p g r u"),
             )
-            return grouped
 
-        def quantize_x(s, j, grouped):
-            cols = slice(j * P, (j + 1) * P)
+        def quantize_x(s, j0, count, grouped):
+            cols = slice(j0 * P, (j0 + count) * P)
             for g in range(PASSES):
                 nc.vector.quantize_mx(
                     out=x_codes[s][:, g, cols].bitcast(E5M2X4), scales=x_scales[s][:, g, cols], in_=grouped[:, g, :]
                 )
 
-        def spread_bias():
+        def spread_bias(chunks):
+            rows = 3 * D // P
             bank = psum.tile([P, BANK], F32, name="mx", tag="mx")
-            nc.tensor.matmul(bank[:, 0:QK_TILES], lhsT=bias_rows[:], rhs=ident_bf[:, 0:QK_TILES], start=True, stop=True)
-            nc.scalar.copy(out=bias_col[:], in_=bank[:, 0:QK_TILES])
-            for c in range(2):
+            nc.tensor.matmul(bank[:, 0:rows], lhsT=bias_rows[:], rhs=ident_bf[:, 0:rows], start=True, stop=True)
+            nc.scalar.copy(out=bias_col[:], in_=bank[:, 0:rows])
+            for c in range(chunks):
                 bank = psum.tile([P, BANK], F32, name="mx", tag="mx")
                 for r in range(4):
                     row = QK_TILES + 4 * c + r
@@ -186,7 +188,7 @@ def tile_attention_pa_kernel(tc, x, W_kqv_words, W_kqv_scales, b_kqv, out_0, out
         biased = {}
 
         def qk_product(n):
-            s, pair = divmod(n, UNITS_PER_SPAN)
+            s, pair = n
             for e in range(2):
                 m = 2 * pair + e
                 bank = psum.tile([P, BANK], F32, name="mx", tag="mx")
@@ -199,7 +201,7 @@ def tile_attention_pa_kernel(tc, x, W_kqv_words, W_kqv_scales, b_kqv, out_0, out
                         rhs=x_codes[s][:, g, :].bitcast(E5M2X4), rhs_scale=x_scales[s][:, g, :],
                         start=(g == 0), stop=(g == PASSES - 1),
                     )
-                biased[n, e] = work.tile([P, BANK], F32, name="biased", tag="biased", bufs=4)
+                biased[n, e] = work.tile([P, BANK], F32, name="biased", tag="biased", bufs=6)
                 nc.scalar.activation(
                     out=biased[n, e][:], in_=bank[:], func=ACT.Identity, bias=bias_col[:, m : m + 1], scale=1.0
                 )
@@ -216,7 +218,7 @@ def tile_attention_pa_kernel(tc, x, W_kqv_words, W_kqv_scales, b_kqv, out_0, out
             return banks
 
         def qk_rotate(n, banks):
-            s, pair = divmod(n, UNITS_PER_SPAN)
+            s, pair = n
             rows = slice(s * SUB, (s + 1) * SUB)
             by_cos = work.tile([P, 4, SUB, DH], F32, name="by_cos", tag="by_cos")
             by_sin = work.tile([P, 4, SUB, DH], F32, name="by_sin", tag="by_sin")
@@ -236,9 +238,9 @@ def tile_attention_pa_kernel(tc, x, W_kqv_words, W_kqv_scales, b_kqv, out_0, out
                 )
             return by_cos, by_sin
 
-        def qk_add(n, by_cos, by_sin, heads):
-            rotated = work.tile([P, 4, SUB * DH], F32, name="rotated", tag="rotated", bufs=4)
-            nc.gpsimd.tensor_tensor(
+        def qk_add(by_cos, by_sin, heads, engine, tag="rotated"):
+            rotated = work.tile([P, 4, SUB * DH], F32, name=tag, tag=tag, bufs=4 if tag == "rotated" else 1, align_bytes=64)
+            engine.tensor_tensor(
                 out=rotated[:, heads, :].rearrange("p h r -> p (h r)"),
                 in0=by_cos[:, heads, :, :].rearrange("p h j f -> p (h j f)"),
                 in1=by_sin[:, heads, :, :].rearrange("p h j f -> p (h j f)"), op=ALU.add,
@@ -246,50 +248,67 @@ def tile_attention_pa_kernel(tc, x, W_kqv_words, W_kqv_scales, b_kqv, out_0, out
             return rotated
 
         def qk_store(n, rotated, heads):
-            s, pair = divmod(n, UNITS_PER_SPAN)
+            s, pair = n
             which, group = divmod(pair, 4)
-            hbm = (out_0, out_1)[which][4 * group : 4 * (group + 1), s * SPAN : (s + 1) * SPAN, :]
+            hbm = (out_0, out_1, out_2)[which][4 * group : 4 * (group + 1), s * SPAN : (s + 1) * SPAN, :]
             nc.sync.dma_start(out=hbm.rearrange("h (p j) f -> p h (j f)", j=SUB)[:, heads, :], in_=rotated[:, heads, :])
 
-        groups = [transpose_x(0, 0), transpose_x(0, 1)]
-        spread_bias()
-        groups += [transpose_x(0, 2), transpose_x(0, 3)]
-        trig_tables()
-        quantize_x(0, 0, groups[0])
-        quantize_x(0, 1, groups[1])
-        v_banks = [v_product(0, 0, 0), v_product(0, 0, 1)]
-        quantize_x(0, 2, groups[2])
-        quantize_x(0, 3, groups[3])
-        v_finish(0, 0, 0, v_banks[0])
-        v_finish(0, 0, 1, v_banks[1])
-        qk_product(0)
-        for j in range(2, SUB):
-            v_finish(0, 0, j, v_product(0, 0, j))
+        def v_copy(n, banks):
+            plain = work.tile([P, 4, SUB * DH], F32, name="plain", tag="plain", bufs=2)
+            for e in range(2):
+                nc.scalar.copy(
+                    out=plain[:, 2 * e : 2 * e + 2, :].rearrange("p h (j f) -> p h j f", f=DH),
+                    in_=banks[e][:].rearrange("p j h f -> p h j f"),
+                )
+            return plain
 
-        units = SPANS * UNITS_PER_SPAN
         all_heads = slice(0, 4)
-        v_in_step = {1: (0, 1, 0), 6: (0, 1, 1), 7: (0, 1, 2), 8: (0, 1, 3),
-                     9: (1, 0, 0), 10: (1, 0, 1), 12: (1, 0, 2), 14: (1, 0, 3)}
-        x_in_step = {2: 0, 3: 1, 4: 2, 5: 3}
-        for n in range(units):
-            if n == 1:
-                qk_product(1)
-            if 0 < n < units - 1:
-                qk_product(n + 1)
-            v_bank = v_product(*v_in_step[n]) if n in v_in_step else None
+        first = [keep.tile([P, PASSES, 4 * P], BF16, name="first%d" % j, align_bytes=64) for j in range(SUB)]
+        second = work.tile([P, PASSES, SUB * 4 * P], BF16, name="second", tag="second", bufs=1, align_bytes=64)
+        for j in range(SUB):
+            transpose_x(0, j, first[j][:])
+        quantize_x(0, 0, 1, first[0])
+        quantize_x(0, 1, 1, first[1])
+        spread_bias(2)
+        trig_tables()
+        quantize_x(0, 2, 1, first[2])
+        quantize_x(0, 3, 1, first[3])
+
+        units = [(s, pair) for s in range(SPANS) for pair in range(UNITS_PER_SPAN)]
+        extras = [None]
+        extras += [("x", j) for j in range(SUB)]
+        extras += [("rows", 0, 0, j) for j in range(SUB)] + [("cols", 1, 8)]
+        extras += [("rows", 0, 1, j) for j in range(SUB)] + [("cols", 1, 9)]
+        extras += [None]
+        quantize_step = SUB + 1
+        qk_product(units[0])
+        for step, n in enumerate(units):
+            kind = extras[step][0] if extras[step] else None
+            what = extras[step][1:] if extras[step] else None
+            last = step + 1 == len(units)
+            if not last:
+                qk_product(units[step + 1])
+            if kind == "cols":
+                qk_product(what)
+            if kind == "rows":
+                v_bank = v_product(*what)
+            if kind == "x":
+                transpose_x(1, what[0], second[:, :, 4 * P * what[0] : 4 * P * (what[0] + 1)])
             banks = qk_turn(n)
-            grouped = transpose_x(1, x_in_step[n]) if n in x_in_step else None
+            if kind == "cols":
+                qk_store(what, v_copy(what, qk_turn(what)), all_heads)
+            if kind == "rows":
+                v_finish(*what, v_bank)
             by_cos, by_sin = qk_rotate(n, banks)
-            if n < units - 1:
-                qk_store(n, qk_add(n, by_cos, by_sin, all_heads), all_heads)
-            if grouped is not None:
-                quantize_x(1, x_in_step[n], grouped)
-            if v_bank is not None:
-                v_finish(*v_in_step[n], v_bank)
-        last = [v_product(1, 1, j) for j in range(SUB)]
+            if step == quantize_step:
+                quantize_x(1, 0, SUB, second)
+                qk_store(n, qk_add(by_cos, by_sin, all_heads, nc.gpsimd, "second"), all_heads)
+            elif not last:
+                qk_store(n, qk_add(by_cos, by_sin, all_heads, nc.gpsimd), all_heads)
+        v_banks = [v_product(1, 1, j) for j in range(SUB)]
         for e in range(2):
             heads = slice(2 * e, 2 * e + 2)
-            rotated = qk_add(units - 1, by_cos, by_sin, heads)
+            rotated = qk_add(by_cos, by_sin, heads, nc.gpsimd)
             for j in range(2 * e, 2 * e + 2):
-                v_finish(1, 1, j, last[j])
-            qk_store(units - 1, rotated, heads)
+                v_finish(1, 1, j, v_banks[j])
+            qk_store(n, rotated, heads)

import math
from contextlib import ExitStack

import concourse.mybir as mybir

S, D, H, DH = 1024, 1024, 16, 64
HALF = DH // 2
FLOPS = 2 * S * D * 3 * D

F32 = mybir.dt.float32
BF16 = mybir.dt.bfloat16
I32 = mybir.dt.int32
U32 = mybir.dt.uint32
U8 = mybir.dt.uint8
E5M2X4 = mybir.dt.float8_e5m2_x4
E2M1X4 = mybir.dt.float4_e2m1fn_x4
ALU = mybir.AluOpType
ACT = mybir.ActivationFunctionType

P = 128
PASSES = D // 512
BANK = 512
SUB = 4
SPAN = P * SUB
SPANS = S // SPAN
W_TILES = 3 * D // BANK
QK_TILES = 2 * D // P
UNITS_PER_SPAN = QK_TILES // 2


def tile_attention_pa_kernel(tc, x, W_kqv_words, W_kqv_scales, b_kqv, out_0, out_1, out_2):
    nc = tc.nc
    with ExitStack() as ctx:
        keep = ctx.enter_context(tc.tile_pool(name="keep", bufs=1))
        work = ctx.enter_context(tc.tile_pool(name="work", bufs=3))
        psum = ctx.enter_context(tc.psum_pool(name="psum", bufs=4))
        ctx.enter_context(tc.manual_schedule())

        offset = keep.tile([P, P], F32, name="offset")
        ident = keep.tile([P, P], F32, name="ident")
        ident_bf = keep.tile([P, P], BF16, name="ident_bf")
        bias_rows = keep.tile([P, P], BF16, name="bias_rows")
        bias_col = keep.tile([P, 3 * D // P], F32, name="bias_col")
        bias_v = keep.tile([P, D], F32, name="bias_v")
        w_scales = keep.tile([P, PASSES, 3 * D], U8, name="w_scales", align_bytes=64)
        w_words = [keep.tile([P, PASSES, 2 * BANK], U8, name="w_words%d" % c, align_bytes=64) for c in range(W_TILES)]
        x_rows = {}
        x_codes = [keep.tile([P, PASSES, SPAN], U32, name="x_codes%d" % s, align_bytes=64) for s in range(SPANS)]
        x_scales = [keep.tile([P, PASSES, SPAN], U8, name="x_scales%d" % s, align_bytes=64) for s in range(SPANS)]
        token = keep.tile([P, SPANS * SUB], F32, name="token")
        turns = keep.tile([P, SPANS * SUB, HALF], F32, name="turns")
        whole = keep.tile([P, SPANS * SUB, HALF], I32, name="whole")
        frac = keep.tile([P, SPANS * SUB, HALF], F32, name="frac")
        folded = keep.tile([P, SPANS * SUB, HALF], F32, name="folded")
        cos_t = keep.tile([P, SPANS * SUB, 2, HALF], F32, name="cos_t")
        sin_t = keep.tile([P, SPANS * SUB, 2, HALF], F32, name="sin_t")

        w_hbm = W_kqv_words.rearrange("g p b -> p g b")

        def load_x(s, j0, count):
            rows = x[s * SPAN : (s + 1) * SPAN, :].rearrange("(p j) k -> p j k", j=SUB)
            loaded = keep.tile([P, count, D], BF16, name="x_rows%d_%d" % (s, j0))
            nc.sync.dma_start(out=loaded[:], in_=rows[:, j0 : j0 + count, :])
            for j in range(count):
                x_rows[s, j0 + j] = loaded[:, j, :]

        def load_w(c):
            nc.sync.dma_start(
                out=w_words[c][:].bitcast(I32), in_=w_hbm[:, :, 2 * BANK * c : 2 * BANK * (c + 1)].bitcast(I32)
            )

        nc.vector.memset(bias_rows[:], 0.0)
        nc.gpsimd.iota(
            offset[:], pattern=[[1, P]], base=0, channel_multiplier=-1, allow_small_or_imprecise_dtypes=True
        )
        nc.gpsimd.iota(
            token[:], pattern=[[SPAN, SPANS], [1, SUB]], base=0, channel_multiplier=SUB,
            allow_small_or_imprecise_dtypes=True,
        )
        for eye in (ident_bf, ident):
            nc.vector.tensor_scalar(out=eye[:], in0=offset[:], scalar1=0.0, scalar2=None, op0=ALU.is_equal)
        nc.vector.memset(w_scales[:].bitcast(I32), 0)
        nc.scalar.dma_start(out=bias_rows[0 : 3 * D // P, :], in_=b_kqv.rearrange("(r c) -> r c", c=P))
        load_x(0, 0, 1)
        load_x(0, 1, 1)
        load_x(0, 2, 2)
        for q in (0, 2, 1, 3):
            nc.sync.dma_start(
                out=w_scales[32 * q : 32 * q + 4, :, :].bitcast(I32),
                in_=W_kqv_scales[:, 4 * q : 4 * q + 4, :].rearrange("g r n -> r g n").bitcast(I32),
            )
        load_w(4)
        load_w(0)
        load_x(1, 0, 2)
        load_x(1, 2, 2)
        load_w(1)
        load_w(5)
        load_w(2)
        load_w(3)

        for i in range(4):
            nc.vector.tensor_scalar(
                out=turns[:, :, i], in0=token[:], scalar1=10000.0 ** (-i / HALF) / (2.0 * math.pi), scalar2=None,
                op0=ALU.mult,
            )
        for i in range(4, HALF, 4):
            nc.vector.tensor_scalar(
                out=turns[:, :, i : i + 4], in0=turns[:, :, 0:4], scalar1=10000.0 ** (-i / HALF), scalar2=None,
                op0=ALU.mult,
            )
        nc.vector.tensor_copy(out=whole[:], in_=turns[:])
        nc.vector.tensor_tensor(out=frac[:], in0=turns[:], in1=whole[:], op=ALU.subtract)
        nc.vector.scalar_tensor_tensor(
            out=folded[:], in0=frac[:], scalar=-1.0, in1=frac[:], op0=ALU.mult, op1=ALU.min
        )
        nc.vector.tensor_scalar(out=folded[:], in0=folded[:], scalar1=0.25, scalar2=None, op0=ALU.add)

        def trig_tables():
            two_pi = 2.0 * math.pi
            nc.scalar.activation(
                out=cos_t[:], in_=folded[:].unsqueeze(2).broadcast_to([P, SPANS * SUB, 2, HALF]),
                func=ACT.Sin, scale=two_pi,
            )
            nc.scalar.activation(out=sin_t[:, :, 0, :], in_=frac[:], func=ACT.Sin, scale=-two_pi)
            nc.scalar.activation(out=sin_t[:, :, 1, :], in_=frac[:], func=ACT.Sin, scale=two_pi)

        def transpose_x(s, j, grouped):
            words = x_rows[s, j].bitcast(F32)
            tag = "tb" if s == 0 else "mx"
            bank = psum.tile([P, PASSES, 2, P], F32, name=tag, tag=tag)
            for g in range(PASSES):
                for u in range(2):
                    nc.tensor.transpose(bank[:, g, u, :], words[:, 256 * g + u : 256 * (g + 1) : 2], ident[:])
            nc.scalar.copy(
                out=grouped.bitcast(F32).rearrange("p g (r u) -> p g r u", u=2),
                in_=bank[:].rearrange("p g u r -> p g r u"),
            )

        def quantize_x(s, j0, count, grouped):
            cols = slice(j0 * P, (j0 + count) * P)
            for g in range(PASSES):
                nc.vector.quantize_mx(
                    out=x_codes[s][:, g, cols].bitcast(E5M2X4), scales=x_scales[s][:, g, cols], in_=grouped[:, g, :]
                )

        def spread_bias(chunks):
            rows = 3 * D // P
            bank = psum.tile([P, BANK], F32, name="mx", tag="mx")
            nc.tensor.matmul(bank[:, 0:rows], lhsT=bias_rows[:], rhs=ident_bf[:, 0:rows], start=True, stop=True)
            nc.scalar.copy(out=bias_col[:], in_=bank[:, 0:rows])
            for c in range(chunks):
                bank = psum.tile([P, BANK], F32, name="mx", tag="mx")
                for r in range(4):
                    row = QK_TILES + 4 * c + r
                    nc.tensor.matmul(
                        bank[:, r * P : (r + 1) * P], lhsT=ident_bf[:, row : row + 1].to_broadcast([P, P]),
                        rhs=bias_rows[:], start=True, stop=True,
                    )
                nc.scalar.copy(out=bias_v[:, c * BANK : (c + 1) * BANK], in_=bank[:])

        v_out = {}

        def v_product(s, c, j):
            bank = psum.tile([P, BANK], F32, name="mx", tag="mx")
            cols = slice(j * P, (j + 1) * P)
            wt = 4 + c
            for g in range(PASSES):
                nc.tensor.matmul_mx(
                    out=bank[:],
                    lhsT=x_codes[s][:, g, cols].bitcast(E5M2X4), lhsT_scale=x_scales[s][:, g, cols],
                    rhs=w_words[wt][:, g, :].bitcast(E2M1X4), rhs_scale=w_scales[:, g, wt * BANK : (wt + 1) * BANK],
                    start=(g == 0), stop=(g == PASSES - 1),
                )
            return bank

        def v_finish(s, c, j, bank):
            if j == 0:
                v_out[s, c] = work.tile([P, 8, SUB, DH], F32, name="v_out", tag="v_out", bufs=2)
            nc.vector.tensor_tensor(
                out=v_out[s, c][:, :, j, :], in0=bank[:].rearrange("p (h f) -> p h f", f=DH),
                in1=bias_v[:, c * BANK : (c + 1) * BANK].rearrange("p (h f) -> p h f", f=DH), op=ALU.add,
            )
            hbm = out_2[8 * c : 8 * (c + 1), s * SPAN : (s + 1) * SPAN, :].rearrange("h (p j) f -> p h (j f)", j=SUB)
            if j % 2 == 1:
                run = slice((j - 1) * DH, (j + 1) * DH)
                nc.sync.dma_start(out=hbm[:, :, run], in_=v_out[s, c][:].rearrange("p h j f -> p h (j f)")[:, :, run])

        biased = {}

        def qk_product(n):
            s, pair = n
            for e in range(2):
                m = 2 * pair + e
                bank = psum.tile([P, BANK], F32, name="mx", tag="mx")
                wt, part = divmod(m, 4)
                for g in range(PASSES):
                    nc.tensor.matmul_mx(
                        out=bank[:],
                        lhsT=w_words[wt][:, g, 2 * P * part : 2 * P * (part + 1)].bitcast(E2M1X4),
                        lhsT_scale=w_scales[:, g, m * P : (m + 1) * P],
                        rhs=x_codes[s][:, g, :].bitcast(E5M2X4), rhs_scale=x_scales[s][:, g, :],
                        start=(g == 0), stop=(g == PASSES - 1),
                    )
                biased[n, e] = work.tile([P, BANK], F32, name="biased", tag="biased", bufs=6)
                nc.scalar.activation(
                    out=biased[n, e][:], in_=bank[:], func=ACT.Identity, bias=bias_col[:, m : m + 1], scale=1.0
                )

        def qk_turn(n):
            banks = []
            for e in range(2):
                bank = psum.tile([P, SUB, 2, DH], F32, name="tb", tag="tb")
                for j in range(SUB):
                    nc.tensor.transpose(
                        bank[:, j, :, :].rearrange("p h f -> p (h f)"), biased[n, e][:, j * P : (j + 1) * P], ident[:]
                    )
                banks.append(bank)
            return banks

        def qk_rotate(n, banks):
            s, pair = n
            rows = slice(s * SUB, (s + 1) * SUB)
            by_cos = work.tile([P, 4, SUB, DH], F32, name="by_cos", tag="by_cos")
            by_sin = work.tile([P, 4, SUB, DH], F32, name="by_sin", tag="by_sin")
            for e in range(2):
                t = banks[e][:].rearrange("p j h f -> p h j f")
                heads = slice(2 * e, 2 * e + 2)
                nc.vector.tensor_tensor(
                    out=by_cos[:, heads, :, :], in0=t,
                    in1=cos_t[:, rows, :, :].rearrange("p j a i -> p j (a i)").unsqueeze(1).broadcast_to([P, 2, SUB, DH]),
                    op=ALU.mult,
                )
                nc.vector.tensor_tensor(
                    out=by_sin[:, heads, :, :].rearrange("p h j (a i) -> p j h a i", a=2),
                    in0=banks[e][:].rearrange("p j h (a i) -> p j h a i", a=2)[:, :, :, ::-1, :],
                    in1=sin_t[:, rows, :, :].unsqueeze(2).broadcast_to([P, SUB, 2, 2, HALF]),
                    op=ALU.mult,
                )
            return by_cos, by_sin

        def qk_add(by_cos, by_sin, heads, engine, tag="rotated"):
            rotated = work.tile([P, 4, SUB * DH], F32, name=tag, tag=tag, bufs=4 if tag == "rotated" else 1, align_bytes=64)
            engine.tensor_tensor(
                out=rotated[:, heads, :].rearrange("p h r -> p (h r)"),
                in0=by_cos[:, heads, :, :].rearrange("p h j f -> p (h j f)"),
                in1=by_sin[:, heads, :, :].rearrange("p h j f -> p (h j f)"), op=ALU.add,
            )
            return rotated

        def qk_store(n, rotated, heads):
            s, pair = n
            which, group = divmod(pair, 4)
            hbm = (out_0, out_1, out_2)[which][4 * group : 4 * (group + 1), s * SPAN : (s + 1) * SPAN, :]
            nc.sync.dma_start(out=hbm.rearrange("h (p j) f -> p h (j f)", j=SUB)[:, heads, :], in_=rotated[:, heads, :])

        def v_copy(n, banks):
            plain = work.tile([P, 4, SUB * DH], F32, name="plain", tag="plain", bufs=2)
            for e in range(2):
                nc.scalar.copy(
                    out=plain[:, 2 * e : 2 * e + 2, :].rearrange("p h (j f) -> p h j f", f=DH),
                    in_=banks[e][:].rearrange("p j h f -> p h j f"),
                )
            return plain

        all_heads = slice(0, 4)
        first = [keep.tile([P, PASSES, 4 * P], BF16, name="first%d" % j, align_bytes=64) for j in range(SUB)]
        second = work.tile([P, PASSES, SUB * 4 * P], BF16, name="second", tag="second", bufs=1, align_bytes=64)
        for j in range(SUB):
            transpose_x(0, j, first[j][:])
        quantize_x(0, 0, 1, first[0])
        quantize_x(0, 1, 1, first[1])
        spread_bias(2)
        trig_tables()
        quantize_x(0, 2, 1, first[2])
        quantize_x(0, 3, 1, first[3])

        units = [(s, pair) for s in range(SPANS) for pair in range(UNITS_PER_SPAN)]
        extras = [None]
        extras += [("x", j) for j in range(SUB)]
        extras += [("rows", 0, 0, j) for j in range(SUB)] + [("cols", 1, 8)]
        extras += [("rows", 0, 1, j) for j in range(SUB)] + [("cols", 1, 9)]
        extras += [None]
        quantize_step = SUB + 1
        qk_product(units[0])
        for step, n in enumerate(units):
            kind = extras[step][0] if extras[step] else None
            what = extras[step][1:] if extras[step] else None
            last = step + 1 == len(units)
            if not last:
                qk_product(units[step + 1])
            if kind == "cols":
                qk_product(what)
            if kind == "rows":
                v_bank = v_product(*what)
            if kind == "x":
                transpose_x(1, what[0], second[:, :, 4 * P * what[0] : 4 * P * (what[0] + 1)])
            banks = qk_turn(n)
            if kind == "cols":
                qk_store(what, v_copy(what, qk_turn(what)), all_heads)
            if kind == "rows":
                v_finish(*what, v_bank)
            by_cos, by_sin = qk_rotate(n, banks)
            if step == quantize_step:
                quantize_x(1, 0, SUB, second)
                qk_store(n, qk_add(by_cos, by_sin, all_heads, nc.gpsimd, "second"), all_heads)
            elif not last:
                qk_store(n, qk_add(by_cos, by_sin, all_heads, nc.gpsimd), all_heads)
        v_banks = [v_product(1, 1, j) for j in range(SUB)]
        for e in range(2):
            heads = slice(2 * e, 2 * e + 2)
            rotated = qk_add(by_cos, by_sin, heads, nc.gpsimd)
            for j in range(2 * e, 2 * e + 2):
                v_finish(1, 1, j, v_banks[j])
            qk_store(n, rotated, heads)
